import numpy as np
import ml_dtypes


def mxq(x, axis, fmt="e4m3"):
    dtype, down = {"e4m3": (ml_dtypes.float8_e4m3fn, 7), "e5m2": (ml_dtypes.float8_e5m2, 14)}[fmt]
    v = np.moveaxis(np.asarray(x, np.float32).astype(ml_dtypes.bfloat16).astype(np.float64), axis, -1)
    blocks = v.reshape(v.shape[:-1] + (-1, 32))
    amax = np.abs(blocks).max(-1, keepdims=True)
    byte = np.maximum(np.where(amax > 0, np.frexp(amax)[1] - 1 + 127, 0) - down, 1)
    scale = np.exp2(byte - 127.0)
    codes = (blocks / scale).astype(np.float32).astype(dtype).astype(np.float64)
    return np.moveaxis((codes * scale).reshape(v.shape), -1, axis)


WIDE = False


def mx_kscale(k):
    if not WIDE:
        return np.ones(k)
    levels = np.array([10, -10, 5, -5, 0])
    a = np.random.permutation(np.resize(levels, k // 512 * 4)).reshape(k // 512, 4)
    idx = np.arange(k)
    return np.exp2(a[idx // 512, idx % 128 // 32])


BF16 = ml_dtypes.bfloat16


def bf(x):
    return np.asarray(x, np.float32).astype(BF16)


def f64(x):
    return np.asarray(x).astype(np.float64)


E2M1 = np.array([0.0, 0.5, 1.0, 1.5, 2.0, 3.0, 4.0, 6.0, -0.0, -0.5, -1.0, -1.5, -2.0, -3.0, -4.0, -6.0])


def pack_weight(w, fmt):
    k, n = w.shape
    w = f64(bf(w)).reshape(k // 32, 32, n)
    amax = np.abs(w).max(1)
    if fmt == "e4m3":
        byte = np.frexp(amax)[1] - 1 + 127 - 7
    else:
        mant, ex = np.frexp(amax / 6.0)
        byte = np.where(mant > 0.5, ex, ex - 1) + 127
    byte = np.clip(np.where(amax > 0, byte, 1), 1, 254)
    scaled = (w * np.exp2(127.0 - byte)[:, None, :]).reshape(k, n).astype(np.float32)
    by_word = np.ascontiguousarray(scaled.reshape(k // 512, 128, 4, n).transpose(0, 1, 3, 2))
    if fmt == "e4m3":
        words = by_word.astype(ml_dtypes.float8_e4m3fn).view(np.uint8)
    else:
        c = by_word.astype(ml_dtypes.float4_e2m1fn).view(np.uint8) & 0xF
        words = c[..., 0::2] | (c[..., 1::2] << 4)
    return np.ascontiguousarray(words), np.ascontiguousarray(byte.astype(np.uint8).reshape(k // 512, 16, n))


def unpack_weight(words, scales, fmt):
    g, p, n, _ = words.shape
    if fmt == "e4m3":
        vals = np.ascontiguousarray(words).view(ml_dtypes.float8_e4m3fn).astype(np.float64)
    else:
        nib = np.empty((g, p, n, 4), np.uint8)
        nib[..., 0::2] = words & 0xF
        nib[..., 1::2] = words >> 4
        vals = E2M1[nib]
    vals = vals * np.repeat(np.exp2(scales.astype(np.float64) - 127.0), 8, axis=1)[..., None]
    return vals.transpose(0, 1, 3, 2).reshape(g * 512, n)

def pack4(w):
    words, scales = pack_weight(w, "e2m1")
    return words.reshape(words.shape[0], 128, -1), scales


def unpack4(words, scales):
    return unpack_weight(words.reshape(words.shape[0], 128, -1, 2), scales, "e2m1")


B, CL, CH, CK, CV, CO, H, W = 2, 8192, 2048, 128, 256, 1024, 24, 24
N = H * W
PSP = (1, 3, 6, 8)
EPS = 1e-5


def psp(x):
    b, c, h, w = x.shape
    return np.concatenate(
        [x.reshape(b, c, s, h // s, s, w // s).mean(axis=(3, 5)).reshape(b, c, s * s) for s in PSP], axis=2)


def setup_inputs():
    s = mx_kscale(CL)
    low_feats = bf(np.random.standard_normal((B, CL, H, W)) * s[None, :, None, None])
    wk = np.random.standard_normal((CK, CL)) * 2.5 / np.sqrt(CL) / s[None, :]
    wk_words, wk_scales = pack4(np.ascontiguousarray(wk.T))
    bk = bf(np.random.standard_normal(CK) * 0.3)
    gk = bf(np.random.uniform(0.5, 1.5, CK))
    bek = bf(np.random.standard_normal(CK) * 0.3)
    mk = bf(np.random.standard_normal(CK) * 0.3)
    vk = bf(np.random.uniform(0.5, 1.5, CK))
    wv = np.random.standard_normal((CV, CL)) * 3.0 / np.sqrt(CL) / s[None, :]
    wv_words, wv_scales = pack4(np.ascontiguousarray(wv.T))
    bv = bf(np.random.standard_normal(CV) * 0.3)
    return {"low_feats": low_feats,
            "wk_words": wk_words,
            "wk_scales": wk_scales,
            "bk": bk,
            "gk": gk,
            "bek": bek,
            "mk": mk,
            "vk": vk,
            "wv_words": wv_words,
            "wv_scales": wv_scales,
            "bv": bv}


def reference(low_feats, wk_words, wk_scales, bk, gk, bek, mk, vk, wv_words, wv_scales, bv):
    xq = mxq(f64(low_feats).reshape(B, CL, N), 1, "e4m3")
    v = (unpack4(wv_words, wv_scales).T @ xq) + f64(bv)[None, :, None]
    value = psp(v.reshape(B, CV, H, W)).transpose(0, 2, 1)
    u = (unpack4(wk_words, wk_scales).T @ xq) + f64(bk)[None, :, None]
    sc = f64(gk) / np.sqrt(f64(vk) + EPS)
    r = np.maximum((u - f64(mk)[None, :, None]) * sc[None, :, None] + f64(bek)[None, :, None], 0.0)
    key = psp(r.reshape(B, CK, H, W))
    return value, key

@@ -1,0 +1,245 @@
+from contextlib import ExitStack
+
+import concourse.mybir as mybir
+from concourse.masks import make_identity
+
+F32 = mybir.dt.float32
+BF16 = mybir.dt.bfloat16
+I32 = mybir.dt.int32
+U32 = mybir.dt.uint32
+U8 = mybir.dt.uint8
+FP8X4 = mybir.dt.float8_e4m3fn_x4
+FP4X4 = mybir.dt.float4_e2m1fn_x4
+ACT = mybir.ActivationFunctionType
+ALU = mybir.AluOpType
+AX = mybir.AxisListType
+
+P = 128
+PACK = 4
+BATCH = 2
+GROUPS = 16
+UNITS = BATCH * GROUPS
+SIDE = 24
+PIX = SIDE * SIDE
+WIDE = 512
+NARROW = 128
+REST = PIX - WIDE
+M_TILES = 3
+KEY = 2
+LOCS = 110
+EPS = 1e-5
+NINTH = 1.0 / 9.0
+
+RUN = 4
+VECTOR_PIX = 240
+X_AHEAD = 3
+W_CHUNK = 2
+RAW_BUFS = 6
+GROUPED_BUFS = 4
+
+FLOPS = 2 * BATCH * PIX * 8192 * (256 + 128)
+
+
+def tile_afnb_pa_k_kernel(
+    tc, low_feats, wk_words, wk_scales, bk, gk, bek, mk, vk, wv_words, wv_scales, bv, out_0, out_1
+):
+    nc = tc.nc
+    x_units = low_feats.rearrange("b (g p j) h w -> (b g) p (j h w)", p=P, j=PACK)
+
+    with ExitStack() as ctx:
+        keep = ctx.enter_context(tc.tile_pool(name="keep", bufs=1))
+        raw_pool = ctx.enter_context(tc.tile_pool(name="raw", bufs=RAW_BUFS))
+        grouped_pool = ctx.enter_context(tc.tile_pool(name="grouped", bufs=GROUPED_BUFS))
+        epi = ctx.enter_context(tc.tile_pool(name="epi", bufs=2))
+        acc_pool = ctx.enter_context(tc.psum_pool(name="acc", bufs=1))
+        turn_pool = ctx.enter_context(tc.psum_pool(name="turn", bufs=2))
+
+        x_codes = keep.tile([P, UNITS * PIX + REST], U32, align_bytes=64)
+        x_scales = keep.tile([P, UNITS * PIX + REST], U8, align_bytes=64)
+        wv_sb = keep.tile([P, GROUPS, 2 * 256], U8, align_bytes=64)
+        wk_sb = keep.tile([P, GROUPS, 2 * 128], U8, align_bytes=64)
+        wv_plane = keep.tile([P, GROUPS, 256], U8, align_bytes=64)
+        wk_plane = keep.tile([P, GROUPS, 128], U8, align_bytes=64)
+
+        raws = {}
+
+        def load_x(u):
+            raw = raw_pool.tile([P, PACK, PIX], BF16, name="raw")
+            nc.sync.dma_start(out=raw[:].rearrange("p j w -> p (j w)"), in_=x_units[u])
+            raws[u] = raw
+
+        def load_scale_rows(plane, scales):
+            rows = scales.rearrange("g (q r) n -> r q g n", r=4)
+            for r in range(4):
+                nc.sync.dma_start(out=plane[r:P:32, :, :].bitcast(I32), in_=rows[r].bitcast(I32))
+
+        def load_weight_words(g0):
+            gs = slice(g0, g0 + W_CHUNK)
+            nc.sync.dma_start(
+                out=wv_sb[:, gs, :].bitcast(I32),
+                in_=wv_words[gs].rearrange("g p n -> p g n").bitcast(I32),
+            )
+            nc.sync.dma_start(
+                out=wk_sb[:, gs, :].bitcast(I32),
+                in_=wk_words[gs].rearrange("g p n -> p g n").bitcast(I32),
+            )
+
+        for u in range(X_AHEAD):
+            load_x(u)
+
+        nc.vector.memset(wv_plane[:].rearrange("p g n -> p (g n)").bitcast(I32), 0)
+        nc.vector.memset(wk_plane[:].rearrange("p g n -> p (g n)").bitcast(I32), 0)
+        nc.vector.memset(x_codes[:, UNITS * PIX :].bitcast(I32), 0)
+        nc.vector.memset(x_scales[:, UNITS * PIX :].bitcast(I32), 0)
+        load_scale_rows(wv_plane, wv_scales)
+        load_scale_rows(wk_plane, wk_scales)
+
+        one = keep.tile([P, 1], F32)
+        nc.vector.memset(one[:], 1.0)
+        nc.scalar.sqrt(out=one[:], in_=one[:])
+
+        ident = keep.tile([P, P], F32)
+        make_identity(nc, ident[:])
+
+        level_factor = keep.tile([P, 46], F32)
+        nc.gpsimd.memset(level_factor[:, 0:1], 9.0 / 576.0)
+        nc.gpsimd.memset(level_factor[:, 1:10], 9.0 / 64.0)
+        nc.gpsimd.memset(level_factor[:, 10:46], 9.0 / 16.0)
+
+        vec_rows = keep.tile([P, P], BF16)
+        nc.gpsimd.memset(vec_rows[:], 0.0)
+        for row, vec in enumerate((bk, gk, bek, mk, vk)):
+            nc.scalar.dma_start(out=vec_rows[row : row + 1, :], in_=vec.rearrange("(o c) -> o c", o=1))
+        nc.scalar.dma_start(out=vec_rows[5:7, :], in_=bv.rearrange("(o c) -> o c", o=2))
+        vec_rows_f32 = keep.tile([P, P], F32)
+        nc.vector.tensor_copy(out=vec_rows_f32[:], in_=vec_rows[:])
+        vec_turned = turn_pool.tile([P, 2 * P], F32, name="turned")
+        nc.tensor.transpose(out=vec_turned[:, 0:P], in_=vec_rows_f32[:], identity=ident[:])
+        cols = keep.tile([P, 8], F32)
+        nc.vector.tensor_copy(out=cols[:], in_=vec_turned[:, 0:8])
+        cols_ninth = keep.tile([P, 8], F32)
+        nc.vector.tensor_scalar_mul(out=cols_ninth[:], in0=cols[:], scalar1=NINTH)
+        std = keep.tile([P, 1], F32)
+        nc.vector.tensor_scalar_add(out=std[:], in0=cols[:, 4:5], scalar1=EPS)
+        nc.scalar.sqrt(out=std[:], in_=std[:])
+        inv_std = keep.tile([P, 1], F32)
+        nc.vector.reciprocal(out=inv_std[:], in_=std[:])
+        key_scale = keep.tile([P, 1], F32)
+        nc.vector.tensor_mul(out=key_scale[:], in0=cols_ninth[:, 1:2], in1=inv_std[:])
+        bk_less_mk = keep.tile([P, 1], F32)
+        nc.vector.tensor_sub(out=bk_less_mk[:], in0=cols[:, 0:1], in1=cols[:, 3:4])
+        key_bias = keep.tile([P, 1], F32)
+        nc.vector.scalar_tensor_tensor(
+            out=key_bias[:], in0=bk_less_mk[:], scalar=key_scale[:, 0:1], in1=cols_ninth[:, 2:3],
+            op0=ALU.mult, op1=ALU.add,
+        )
+
+        groupeds = {}
+
+        def regroup(u):
+            raw = raws[u]
+            grouped = grouped_pool.tile([P, PIX, PACK], BF16, name="grouped", align_bytes=64)
+            src = raw[:].rearrange("p j (c i) -> p c j i", i=RUN)
+            dst = grouped[:].rearrange("p (c i) j -> p c j i", i=RUN)
+            cut = VECTOR_PIX // RUN
+            nc.vector.tensor_copy(out=dst[:, :cut], in_=src[:, :cut])
+            nc.scalar.copy(out=dst[:, cut:], in_=src[:, cut:])
+            groupeds[u] = grouped
+
+        def quantise(u):
+            flat = groupeds[u][:].rearrange("p w j -> p (w j)")
+            for lo, hi in ((0, WIDE), (WIDE, PIX)):
+                nc.vector.quantize_mx(
+                    out=x_codes[:, u * PIX + lo : u * PIX + hi].bitcast(FP8X4),
+                    scales=x_scales[:, u * PIX + lo : u * PIX + hi],
+                    in_=flat[:, PACK * lo : PACK * hi],
+                )
+
+        def weights(m, g):
+            if m == KEY:
+                return wk_sb[:, g, :].bitcast(FP4X4), wk_plane[:, g, :]
+            return (
+                wv_sb[:, g, 2 * P * m : 2 * P * (m + 1)].bitcast(FP4X4),
+                wv_plane[:, g, P * m : P * (m + 1)],
+            )
+
+        accs = {}
+
+        def multiply(u, first_col, width, kind):
+            g = u % GROUPS
+            cols_of_x = slice(u * PIX + first_col, u * PIX + first_col + width)
+            for m in range(M_TILES):
+                if g == 0:
+                    accs[kind, m] = acc_pool.tile([P, WIDE], F32, name="acc_%s%d" % (kind, m))
+                words, plane = weights(m, g)
+                nc.tensor.matmul_mx(
+                    out=accs[kind, m][:, 0:width],
+                    lhsT=words,
+                    lhsT_scale=plane,
+                    rhs=x_codes[:, cols_of_x].bitcast(FP8X4),
+                    rhs_scale=x_scales[:, cols_of_x],
+                    start=(g == 0),
+                    stop=(g == GROUPS - 1),
+                )
+
+        def finish_image(b):
+            store_queue = nc.sync if b == BATCH - 1 else nc.gpsimd
+            full = epi.tile([P, M_TILES, PIX], F32, name="full")
+            pooled = epi.tile([P, M_TILES, P], F32, name="pooled")
+            nc.gpsimd.memset(pooled[:], 0.0)
+            for m in range(M_TILES):
+                for dst, src in (
+                    (full[:, m, 0:WIDE], accs["wide", m][:, :]),
+                    (full[:, m, WIDE:PIX], accs["narrow", m][:, 0:REST]),
+                ):
+                    if m == KEY:
+                        nc.scalar.activation(
+                            out=dst, in_=src, func=ACT.Relu, bias=key_bias[:, 0:1], scale=key_scale[:, 0:1]
+                        )
+                    else:
+                        nc.scalar.activation(
+                            out=dst, in_=src, func=ACT.Identity, bias=cols_ninth[:, 5 + m : 6 + m], scale=NINTH
+                        )
+                nc.vector.tensor_reduce(
+                    out=pooled[:, m, 46:110].rearrange("p (hb wb) -> p hb wb", hb=8),
+                    in_=full[:, m, :].rearrange("p (hb hi wb wi) -> p hb wb hi wi", hb=8, hi=3, wb=8, wi=3),
+                    axis=AX.XY, op=ALU.add,
+                )
+                nc.vector.tensor_reduce(
+                    out=pooled[:, m, 10:46].rearrange("p (hb wb) -> p hb wb", hb=6),
+                    in_=full[:, m, :].rearrange("p (hb hi wb wi) -> p hb wb hi wi", hb=6, hi=4, wb=6, wi=4),
+                    axis=AX.XY, op=ALU.add,
+                )
+                nc.vector.tensor_reduce(
+                    out=pooled[:, m, 1:10].rearrange("p (hb wb) -> p hb wb", hb=3),
+                    in_=pooled[:, m, 10:46].rearrange("p (hb hi wb wi) -> p hb wb hi wi", hb=3, hi=2, wb=3, wi=2),
+                    axis=AX.XY, op=ALU.add,
+                )
+                nc.vector.tensor_reduce(
+                    out=pooled[:, m, 0:1], in_=pooled[:, m, 1:10], axis=AX.X, op=ALU.add
+                )
+                nc.vector.tensor_mul(out=pooled[:, m, 0:46], in0=pooled[:, m, 0:46], in1=level_factor[:])
+            turned = turn_pool.tile([P, 2 * P], F32, name="turned")
+            for m in range(KEY):
+                nc.tensor.transpose(out=turned[:, P * m : P * (m + 1)], in_=pooled[:, m, :], identity=ident[:])
+            value_sb = epi.tile([P, 2 * P], F32, name="value_sb")
+            nc.scalar.copy(out=value_sb[:], in_=turned[:])
+            store_queue.dma_start(out=out_0[b], in_=value_sb[0:LOCS, :])
+            store_queue.dma_start(out=out_1[b], in_=pooled[:, KEY, 0:LOCS])
+
+        for step in range(UNITS + 2):
+            ask = step + X_AHEAD
+            if ask < UNITS:
+                if step % W_CHUNK == 0 and step < GROUPS:
+                    load_weight_words(step)
+                load_x(ask)
+            if step < UNITS:
+                regroup(step)
+            if 1 <= step <= UNITS:
+                quantise(step - 1)
+            if step >= 2:
+                multiply(step - 2, WIDE, NARROW, "narrow")
+                if (step - 2) % GROUPS == GROUPS - 1:
+                    finish_image((step - 2) // GROUPS)
+            if 1 <= step <= UNITS:
+                multiply(step - 1, 0, WIDE, "wide")

@@ -32,10 +32,12 @@ NINTH = 1.0 / 9.0
 
 RUN = 4
 VECTOR_PIX = 240
-X_AHEAD = 3
-W_CHUNK = 2
 RAW_BUFS = 6
+X_AHEAD = RAW_BUFS - 1
 GROUPED_BUFS = 4
+W_CHUNK = 2
+PE_LAG = 2
+BANKS = 8
 
 FLOPS = 2 * BATCH * PIX * 8192 * (256 + 128)
 
@@ -51,8 +53,8 @@ def tile_afnb_pa_k_kernel(
         raw_pool = ctx.enter_context(tc.tile_pool(name="raw", bufs=RAW_BUFS))
         grouped_pool = ctx.enter_context(tc.tile_pool(name="grouped", bufs=GROUPED_BUFS))
         epi = ctx.enter_context(tc.tile_pool(name="epi", bufs=2))
-        acc_pool = ctx.enter_context(tc.psum_pool(name="acc", bufs=1))
-        turn_pool = ctx.enter_context(tc.psum_pool(name="turn", bufs=2))
+        psum = ctx.enter_context(tc.psum_pool(name="psum", bufs=BANKS))
+        ctx.enter_context(tc.manual_schedule())
 
         x_codes = keep.tile([P, UNITS * PIX + REST], U32, align_bytes=64)
         x_scales = keep.tile([P, UNITS * PIX + REST], U8, align_bytes=64)
@@ -84,19 +86,22 @@ def tile_afnb_pa_k_kernel(
                 in_=wk_words[gs].rearrange("g p n -> p g n").bitcast(I32),
             )
 
+        vec_rows = keep.tile([P, P], BF16)
+        nc.gpsimd.memset(vec_rows[:], 0.0)
+        for row, vec in enumerate((bk, gk, bek, mk, vk)):
+            nc.scalar.dma_start(out=vec_rows[row : row + 1, :], in_=vec.rearrange("(o c) -> o c", o=1))
+        nc.scalar.dma_start(out=vec_rows[5:7, :], in_=bv.rearrange("(o c) -> o c", o=2))
         for u in range(X_AHEAD):
             load_x(u)
+
+        one = keep.tile([P, 1], F32)
+        nc.vector.memset(one[:], 1.0)
+        nc.scalar.sqrt(out=one[:], in_=one[:])
 
         nc.vector.memset(wv_plane[:].rearrange("p g n -> p (g n)").bitcast(I32), 0)
         nc.vector.memset(wk_plane[:].rearrange("p g n -> p (g n)").bitcast(I32), 0)
         nc.vector.memset(x_codes[:, UNITS * PIX :].bitcast(I32), 0)
         nc.vector.memset(x_scales[:, UNITS * PIX :].bitcast(I32), 0)
-        load_scale_rows(wv_plane, wv_scales)
-        load_scale_rows(wk_plane, wk_scales)
-
-        one = keep.tile([P, 1], F32)
-        nc.vector.memset(one[:], 1.0)
-        nc.scalar.sqrt(out=one[:], in_=one[:])
 
         ident = keep.tile([P, P], F32)
         make_identity(nc, ident[:])
@@ -106,33 +111,40 @@ def tile_afnb_pa_k_kernel(
         nc.gpsimd.memset(level_factor[:, 1:10], 9.0 / 64.0)
         nc.gpsimd.memset(level_factor[:, 10:46], 9.0 / 16.0)
 
-        vec_rows = keep.tile([P, P], BF16)
-        nc.gpsimd.memset(vec_rows[:], 0.0)
-        for row, vec in enumerate((bk, gk, bek, mk, vk)):
-            nc.scalar.dma_start(out=vec_rows[row : row + 1, :], in_=vec.rearrange("(o c) -> o c", o=1))
-        nc.scalar.dma_start(out=vec_rows[5:7, :], in_=bv.rearrange("(o c) -> o c", o=2))
-        vec_rows_f32 = keep.tile([P, P], F32)
-        nc.vector.tensor_copy(out=vec_rows_f32[:], in_=vec_rows[:])
-        vec_turned = turn_pool.tile([P, 2 * P], F32, name="turned")
-        nc.tensor.transpose(out=vec_turned[:, 0:P], in_=vec_rows_f32[:], identity=ident[:])
         cols = keep.tile([P, 8], F32)
-        nc.vector.tensor_copy(out=cols[:], in_=vec_turned[:, 0:8])
         cols_ninth = keep.tile([P, 8], F32)
-        nc.vector.tensor_scalar_mul(out=cols_ninth[:], in0=cols[:], scalar1=NINTH)
         std = keep.tile([P, 1], F32)
-        nc.vector.tensor_scalar_add(out=std[:], in0=cols[:, 4:5], scalar1=EPS)
-        nc.scalar.sqrt(out=std[:], in_=std[:])
-        inv_std = keep.tile([P, 1], F32)
-        nc.vector.reciprocal(out=inv_std[:], in_=std[:])
         key_scale = keep.tile([P, 1], F32)
-        nc.vector.tensor_mul(out=key_scale[:], in0=cols_ninth[:, 1:2], in1=inv_std[:])
-        bk_less_mk = keep.tile([P, 1], F32)
-        nc.vector.tensor_sub(out=bk_less_mk[:], in0=cols[:, 0:1], in1=cols[:, 3:4])
         key_bias = keep.tile([P, 1], F32)
-        nc.vector.scalar_tensor_tensor(
-            out=key_bias[:], in0=bk_less_mk[:], scalar=key_scale[:, 0:1], in1=cols_ninth[:, 2:3],
-            op0=ALU.mult, op1=ALU.add,
-        )
+        vec_turned = psum.tile([P, WIDE], F32, name="bank")
+
+        def turn_vectors():
+            vec_rows_f32 = keep.tile([P, P], F32)
+            nc.vector.tensor_copy(out=vec_rows_f32[:], in_=vec_rows[:])
+            nc.tensor.transpose(out=vec_turned[:, 0:P], in_=vec_rows_f32[:], identity=ident[:])
+
+        def start_key_scale():
+            nc.vector.tensor_copy(out=cols[:], in_=vec_turned[:, 0:8])
+            nc.vector.tensor_scalar_mul(out=cols_ninth[:], in0=cols[:], scalar1=NINTH)
+            nc.vector.tensor_scalar_add(out=std[:], in0=cols[:, 4:5], scalar1=EPS)
+            nc.scalar.sqrt(out=std[:], in_=std[:])
+
+        def finish_key_scale():
+            inv_std = keep.tile([P, 1], F32)
+            nc.vector.reciprocal(out=inv_std[:], in_=std[:])
+            nc.vector.tensor_mul(out=key_scale[:], in0=cols_ninth[:, 1:2], in1=inv_std[:])
+            bk_less_mk = keep.tile([P, 1], F32)
+            nc.vector.tensor_sub(out=bk_less_mk[:], in0=cols[:, 0:1], in1=cols[:, 3:4])
+            nc.vector.scalar_tensor_tensor(
+                out=key_bias[:], in0=bk_less_mk[:], scalar=key_scale[:, 0:1], in1=cols_ninth[:, 2:3],
+                op0=ALU.mult, op1=ALU.add,
+            )
+
+        pooleds = []
+        for b in range(BATCH):
+            pooled = keep.tile([P, M_TILES, P], F32, name="pooled%d" % b)
+            nc.gpsimd.memset(pooled[:], 0.0)
+            pooleds.append(pooled)
 
         groupeds = {}
 
@@ -165,12 +177,15 @@ def tile_afnb_pa_k_kernel(
 
         accs = {}
 
+        def open_banks():
+            for m in range(M_TILES):
+                for kind in ("wide", "narrow"):
+                    accs[kind, m] = psum.tile([P, WIDE], F32, name="bank")
+
         def multiply(u, first_col, width, kind):
             g = u % GROUPS
             cols_of_x = slice(u * PIX + first_col, u * PIX + first_col + width)
             for m in range(M_TILES):
-                if g == 0:
-                    accs[kind, m] = acc_pool.tile([P, WIDE], F32, name="acc_%s%d" % (kind, m))
                 words, plane = weights(m, g)
                 nc.tensor.matmul_mx(
                     out=accs[kind, m][:, 0:width],
@@ -182,11 +197,11 @@ def tile_afnb_pa_k_kernel(
                     stop=(g == GROUPS - 1),
                 )
 
-        def finish_image(b):
-            store_queue = nc.sync if b == BATCH - 1 else nc.gpsimd
+        fulls = {}
+        turneds = {}
+
+        def leave_psum(b):
             full = epi.tile([P, M_TILES, PIX], F32, name="full")
-            pooled = epi.tile([P, M_TILES, P], F32, name="pooled")
-            nc.gpsimd.memset(pooled[:], 0.0)
             for m in range(M_TILES):
                 for dst, src in (
                     (full[:, m, 0:WIDE], accs["wide", m][:, :]),
@@ -200,46 +215,76 @@ def tile_afnb_pa_k_kernel(
                         nc.scalar.activation(
                             out=dst, in_=src, func=ACT.Identity, bias=cols_ninth[:, 5 + m : 6 + m], scale=NINTH
                         )
-                nc.vector.tensor_reduce(
-                    out=pooled[:, m, 46:110].rearrange("p (hb wb) -> p hb wb", hb=8),
-                    in_=full[:, m, :].rearrange("p (hb hi wb wi) -> p hb wb hi wi", hb=8, hi=3, wb=8, wi=3),
-                    axis=AX.XY, op=ALU.add,
-                )
-                nc.vector.tensor_reduce(
-                    out=pooled[:, m, 10:46].rearrange("p (hb wb) -> p hb wb", hb=6),
-                    in_=full[:, m, :].rearrange("p (hb hi wb wi) -> p hb wb hi wi", hb=6, hi=4, wb=6, wi=4),
-                    axis=AX.XY, op=ALU.add,
-                )
-                nc.vector.tensor_reduce(
-                    out=pooled[:, m, 1:10].rearrange("p (hb wb) -> p hb wb", hb=3),
-                    in_=pooled[:, m, 10:46].rearrange("p (hb hi wb wi) -> p hb wb hi wi", hb=3, hi=2, wb=3, wi=2),
-                    axis=AX.XY, op=ALU.add,
-                )
-                nc.vector.tensor_reduce(
-                    out=pooled[:, m, 0:1], in_=pooled[:, m, 1:10], axis=AX.X, op=ALU.add
-                )
-                nc.vector.tensor_mul(out=pooled[:, m, 0:46], in0=pooled[:, m, 0:46], in1=level_factor[:])
-            turned = turn_pool.tile([P, 2 * P], F32, name="turned")
-            for m in range(KEY):
-                nc.tensor.transpose(out=turned[:, P * m : P * (m + 1)], in_=pooled[:, m, :], identity=ident[:])
-            value_sb = epi.tile([P, 2 * P], F32, name="value_sb")
-            nc.scalar.copy(out=value_sb[:], in_=turned[:])
-            store_queue.dma_start(out=out_0[b], in_=value_sb[0:LOCS, :])
-            store_queue.dma_start(out=out_1[b], in_=pooled[:, KEY, 0:LOCS])
+            fulls[b] = full
 
-        for step in range(UNITS + 2):
-            ask = step + X_AHEAD
-            if ask < UNITS:
-                if step % W_CHUNK == 0 and step < GROUPS:
-                    load_weight_words(step)
-                load_x(ask)
+        def pool(b, m):
+            image = fulls[b][:, m, :]
+            pooled = pooleds[b]
+            nc.vector.tensor_reduce(
+                out=pooled[:, m, 46:110].rearrange("p (hb wb) -> p hb wb", hb=8),
+                in_=image.rearrange("p (hb hi wb wi) -> p hb wb hi wi", hb=8, hi=3, wb=8, wi=3),
+                axis=AX.XY, op=ALU.add,
+            )
+            nc.vector.tensor_reduce(
+                out=pooled[:, m, 10:46].rearrange("p (hb wb) -> p hb wb", hb=6),
+                in_=image.rearrange("p (hb hi wb wi) -> p hb wb hi wi", hb=6, hi=4, wb=6, wi=4),
+                axis=AX.XY, op=ALU.add,
+            )
+            nc.vector.tensor_reduce(
+                out=pooled[:, m, 1:10].rearrange("p (hb wb) -> p hb wb", hb=3),
+                in_=pooled[:, m, 10:46].rearrange("p (hb hi wb wi) -> p hb wb hi wi", hb=3, hi=2, wb=3, wi=2),
+                axis=AX.XY, op=ALU.add,
+            )
+            nc.vector.tensor_reduce(out=pooled[:, m, 0:1], in_=pooled[:, m, 1:10], axis=AX.X, op=ALU.add)
+            nc.vector.tensor_mul(out=pooled[:, m, 0:46], in0=pooled[:, m, 0:46], in1=level_factor[:])
+
+        def turn_value(b):
+            turned = psum.tile([P, WIDE], F32, name="bank")
+            for m in range(KEY):
+                nc.tensor.transpose(
+                    out=turned[:, P * m : P * (m + 1)], in_=pooleds[b][:, m, :], identity=ident[:]
+                )
+            turneds[b] = turned
+
+        def store(b):
+            store_queue = nc.sync if b == BATCH - 1 else nc.gpsimd
+            value_sb = epi.tile([P, 2 * P], F32, name="value_sb")
+            nc.scalar.copy(out=value_sb[:], in_=turneds[b][:, 0 : 2 * P])
+            store_queue.dma_start(out=out_0[b], in_=value_sb[0:LOCS, :])
+            store_queue.dma_start(out=out_1[b], in_=pooleds[b][:, KEY, 0:LOCS])
+
+        def epilogue_pieces(b):
+            return (
+                [lambda: leave_psum(b)]
+                + [lambda m=m: pool(b, m) for m in range(M_TILES)]
+                + [lambda: turn_value(b), lambda: store(b)]
+            )
+
+        pieces = [turn_vectors, start_key_scale, finish_key_scale]
+        for step in range(UNITS + PE_LAG + 2):
+            if step == PE_LAG:
+                load_scale_rows(wv_plane, wv_scales)
+                load_scale_rows(wk_plane, wk_scales)
+            first_group = step - PE_LAG
+            if 0 <= first_group < GROUPS and first_group % W_CHUNK == 0:
+                load_weight_words(first_group)
+            if step + X_AHEAD < UNITS:
+                load_x(step + X_AHEAD)
             if step < UNITS:
                 regroup(step)
             if 1 <= step <= UNITS:
                 quantise(step - 1)
-            if step >= 2:
-                multiply(step - 2, WIDE, NARROW, "narrow")
-                if (step - 2) % GROUPS == GROUPS - 1:
-                    finish_image((step - 2) // GROUPS)
-            if 1 <= step <= UNITS:
-                multiply(step - 1, 0, WIDE, "wide")
+            narrow_unit = step - PE_LAG - 2
+            wide_unit = step - PE_LAG - 1
+            if 0 <= narrow_unit:
+                multiply(narrow_unit, WIDE, NARROW, "narrow")
+                if narrow_unit % GROUPS == GROUPS - 1:
+                    pieces = epilogue_pieces(narrow_unit // GROUPS)
+            if pieces:
+                pieces.pop(0)()
+            if 0 <= wide_unit < UNITS:
+                if wide_unit % GROUPS == 0:
+                    open_banks()
+                multiply(wide_unit, 0, WIDE, "wide")
+        for piece in pieces:
+            piece()

@@ -23,20 +23,18 @@ SIDE = 24
 PIX = SIDE * SIDE
 WIDE = 512
 NARROW = 128
-REST = PIX - WIDE
-M_TILES = 3
-KEY = 2
+NARROW_FROM = PIX - NARROW
+TILES = ("key", "value_low", "value_high")
 LOCS = 110
 EPS = 1e-5
 NINTH = 1.0 / 9.0
 
 RUN = 4
-VECTOR_PIX = 240
+VECTOR_PIX = 256
 RAW_BUFS = 6
 X_AHEAD = RAW_BUFS - 1
 GROUPED_BUFS = 4
 W_CHUNK = 2
-PE_LAG = 2
 BANKS = 8
 
 FLOPS = 2 * BATCH * PIX * 8192 * (256 + 128)
@@ -56,19 +54,12 @@ def tile_afnb_pa_k_kernel(
         psum = ctx.enter_context(tc.psum_pool(name="psum", bufs=BANKS))
         ctx.enter_context(tc.manual_schedule())
 
-        x_codes = keep.tile([P, UNITS * PIX + REST], U32, align_bytes=64)
-        x_scales = keep.tile([P, UNITS * PIX + REST], U8, align_bytes=64)
+        x_codes = keep.tile([P, UNITS, PIX], U32, align_bytes=64)
+        x_scales = keep.tile([P, UNITS, PIX], U8, align_bytes=64)
         wv_sb = keep.tile([P, GROUPS, 2 * 256], U8, align_bytes=64)
         wk_sb = keep.tile([P, GROUPS, 2 * 128], U8, align_bytes=64)
         wv_plane = keep.tile([P, GROUPS, 256], U8, align_bytes=64)
         wk_plane = keep.tile([P, GROUPS, 128], U8, align_bytes=64)
-
-        raws = {}
-
-        def load_x(u):
-            raw = raw_pool.tile([P, PACK, PIX], BF16, name="raw")
-            nc.sync.dma_start(out=raw[:].rearrange("p j w -> p (j w)"), in_=x_units[u])
-            raws[u] = raw
 
         def load_scale_rows(plane, scales):
             rows = scales.rearrange("g (q r) n -> r q g n", r=4)
@@ -86,30 +77,42 @@ def tile_afnb_pa_k_kernel(
                 in_=wk_words[gs].rearrange("g p n -> p g n").bitcast(I32),
             )
 
+        raws = {}
+
+        def ask(u):
+            raw = raw_pool.tile([P, PACK, PIX], BF16, name="raw")
+            nc.sync.dma_start(out=raw[:].rearrange("p j w -> p (j w)"), in_=x_units[u])
+            raws[u] = raw
+            if u == 0:
+                load_scale_rows(wv_plane, wv_scales)
+            if u == 1:
+                load_scale_rows(wk_plane, wk_scales)
+            if u < GROUPS and u % W_CHUNK == 0:
+                load_weight_words(u)
+
         vec_rows = keep.tile([P, P], BF16)
         nc.gpsimd.memset(vec_rows[:], 0.0)
         for row, vec in enumerate((bk, gk, bek, mk, vk)):
-            nc.scalar.dma_start(out=vec_rows[row : row + 1, :], in_=vec.rearrange("(o c) -> o c", o=1))
-        nc.scalar.dma_start(out=vec_rows[5:7, :], in_=bv.rearrange("(o c) -> o c", o=2))
+            nc.gpsimd.dma_start(out=vec_rows[row : row + 1, :], in_=vec.rearrange("(o c) -> o c", o=1))
+        nc.gpsimd.dma_start(out=vec_rows[5:7, :], in_=bv.rearrange("(o c) -> o c", o=2))
+
+        nc.vector.memset(wv_plane[:].rearrange("p g n -> p (g n)").bitcast(I32), 0)
+        nc.vector.memset(wk_plane[:].rearrange("p g n -> p (g n)").bitcast(I32), 0)
         for u in range(X_AHEAD):
-            load_x(u)
+            ask(u)
 
         one = keep.tile([P, 1], F32)
         nc.vector.memset(one[:], 1.0)
         nc.scalar.sqrt(out=one[:], in_=one[:])
 
-        nc.vector.memset(wv_plane[:].rearrange("p g n -> p (g n)").bitcast(I32), 0)
-        nc.vector.memset(wk_plane[:].rearrange("p g n -> p (g n)").bitcast(I32), 0)
-        nc.vector.memset(x_codes[:, UNITS * PIX :].bitcast(I32), 0)
-        nc.vector.memset(x_scales[:, UNITS * PIX :].bitcast(I32), 0)
-
         ident = keep.tile([P, P], F32)
         make_identity(nc, ident[:])
 
-        level_factor = keep.tile([P, 46], F32)
-        nc.gpsimd.memset(level_factor[:, 0:1], 9.0 / 576.0)
-        nc.gpsimd.memset(level_factor[:, 1:10], 9.0 / 64.0)
-        nc.gpsimd.memset(level_factor[:, 10:46], 9.0 / 16.0)
+        pooleds = []
+        for b in range(BATCH):
+            pooled = keep.tile([P, len(TILES), P], F32, name="pooled%d" % b)
+            nc.gpsimd.memset(pooled[:], 0.0)
+            pooleds.append(pooled)
 
         cols = keep.tile([P, 8], F32)
         cols_ninth = keep.tile([P, 8], F32)
@@ -140,18 +143,11 @@ def tile_afnb_pa_k_kernel(
                 op0=ALU.mult, op1=ALU.add,
             )
 
-        pooleds = []
-        for b in range(BATCH):
-            pooled = keep.tile([P, M_TILES, P], F32, name="pooled%d" % b)
-            nc.gpsimd.memset(pooled[:], 0.0)
-            pooleds.append(pooled)
-
         groupeds = {}
 
         def regroup(u):
-            raw = raws[u]
             grouped = grouped_pool.tile([P, PIX, PACK], BF16, name="grouped", align_bytes=64)
-            src = raw[:].rearrange("p j (c i) -> p c j i", i=RUN)
+            src = raws[u][:].rearrange("p j (c i) -> p c j i", i=RUN)
             dst = grouped[:].rearrange("p (c i) j -> p c j i", i=RUN)
             cut = VECTOR_PIX // RUN
             nc.vector.tensor_copy(out=dst[:, :cut], in_=src[:, :cut])
@@ -162,87 +158,95 @@ def tile_afnb_pa_k_kernel(
             flat = groupeds[u][:].rearrange("p w j -> p (w j)")
             for lo, hi in ((0, WIDE), (WIDE, PIX)):
                 nc.vector.quantize_mx(
-                    out=x_codes[:, u * PIX + lo : u * PIX + hi].bitcast(FP8X4),
-                    scales=x_scales[:, u * PIX + lo : u * PIX + hi],
+                    out=x_codes[:, u, lo:hi].bitcast(FP8X4),
+                    scales=x_scales[:, u, lo:hi],
                     in_=flat[:, PACK * lo : PACK * hi],
                 )
 
-        def weights(m, g):
-            if m == KEY:
+        def weights(name, g):
+            if name == "key":
                 return wk_sb[:, g, :].bitcast(FP4X4), wk_plane[:, g, :]
+            half = TILES.index(name) - 1
             return (
-                wv_sb[:, g, 2 * P * m : 2 * P * (m + 1)].bitcast(FP4X4),
-                wv_plane[:, g, P * m : P * (m + 1)],
+                wv_sb[:, g, 2 * P * half : 2 * P * (half + 1)].bitcast(FP4X4),
+                wv_plane[:, g, P * half : P * (half + 1)],
             )
 
-        accs = {}
+        sums = {}
 
-        def open_banks():
-            for m in range(M_TILES):
-                for kind in ("wide", "narrow"):
-                    accs[kind, m] = psum.tile([P, WIDE], F32, name="bank")
-
-        def multiply(u, first_col, width, kind):
-            g = u % GROUPS
-            cols_of_x = slice(u * PIX + first_col, u * PIX + first_col + width)
-            for m in range(M_TILES):
-                words, plane = weights(m, g)
-                nc.tensor.matmul_mx(
-                    out=accs[kind, m][:, 0:width],
-                    lhsT=words,
-                    lhsT_scale=plane,
-                    rhs=x_codes[:, cols_of_x].bitcast(FP8X4),
-                    rhs_scale=x_scales[:, cols_of_x],
-                    start=(g == 0),
-                    stop=(g == GROUPS - 1),
-                )
+        def multiply(u):
+            b, g = divmod(u, GROUPS)
+            for name in TILES:
+                words, plane = weights(name, g)
+                for window, first, width in (("wide", 0, WIDE), ("narrow", NARROW_FROM, NARROW)):
+                    if g == 0:
+                        sums[b, name, window] = psum.tile([P, WIDE], F32, name="bank")
+                    nc.tensor.matmul_mx(
+                        out=sums[b, name, window][:, 0:width],
+                        lhsT=words,
+                        lhsT_scale=plane,
+                        rhs=x_codes[:, u, first : first + width].bitcast(FP8X4),
+                        rhs_scale=x_scales[:, u, first : first + width],
+                        start=(g == 0),
+                        stop=(g == GROUPS - 1),
+                    )
 
         fulls = {}
-        turneds = {}
 
         def leave_psum(b):
-            full = epi.tile([P, M_TILES, PIX], F32, name="full")
-            for m in range(M_TILES):
+            full = epi.tile([P, len(TILES), PIX], F32, name="full")
+            for m, name in enumerate(TILES):
                 for dst, src in (
-                    (full[:, m, 0:WIDE], accs["wide", m][:, :]),
-                    (full[:, m, WIDE:PIX], accs["narrow", m][:, 0:REST]),
+                    (full[:, m, 0:WIDE], sums[b, name, "wide"][:, 0:WIDE]),
+                    (full[:, m, WIDE:PIX], sums[b, name, "narrow"][:, WIDE - NARROW_FROM : NARROW]),
                 ):
-                    if m == KEY:
+                    if name == "key":
                         nc.scalar.activation(
                             out=dst, in_=src, func=ACT.Relu, bias=key_bias[:, 0:1], scale=key_scale[:, 0:1]
                         )
                     else:
                         nc.scalar.activation(
-                            out=dst, in_=src, func=ACT.Identity, bias=cols_ninth[:, 5 + m : 6 + m], scale=NINTH
+                            out=dst, in_=src, func=ACT.Identity, bias=cols_ninth[:, 4 + m : 5 + m], scale=NINTH
                         )
             fulls[b] = full
 
-        def pool(b, m):
+        sums6 = {}
+
+        def pool_blocks(b, m):
+            if m == 0:
+                sums6[b] = epi.tile([P, len(TILES), 36], F32, name="sums6")
             image = fulls[b][:, m, :]
-            pooled = pooleds[b]
             nc.vector.tensor_reduce(
-                out=pooled[:, m, 46:110].rearrange("p (hb wb) -> p hb wb", hb=8),
+                out=pooleds[b][:, m, 46:110].rearrange("p (hb wb) -> p hb wb", hb=8),
                 in_=image.rearrange("p (hb hi wb wi) -> p hb wb hi wi", hb=8, hi=3, wb=8, wi=3),
                 axis=AX.XY, op=ALU.add,
             )
             nc.vector.tensor_reduce(
-                out=pooled[:, m, 10:46].rearrange("p (hb wb) -> p hb wb", hb=6),
+                out=sums6[b][:, m, :].rearrange("p (hb wb) -> p hb wb", hb=6),
                 in_=image.rearrange("p (hb hi wb wi) -> p hb wb hi wi", hb=6, hi=4, wb=6, wi=4),
                 axis=AX.XY, op=ALU.add,
             )
+
+        def pool_coarse(b):
+            sums3 = epi.tile([P, len(TILES), 9], F32, name="sums3")
+            sums1 = epi.tile([P, len(TILES), 1], F32, name="sums1")
             nc.vector.tensor_reduce(
-                out=pooled[:, m, 1:10].rearrange("p (hb wb) -> p hb wb", hb=3),
-                in_=pooled[:, m, 10:46].rearrange("p (hb hi wb wi) -> p hb wb hi wi", hb=3, hi=2, wb=3, wi=2),
+                out=sums3[:].rearrange("p m (hb wb) -> p (m hb) wb", hb=3),
+                in_=sums6[b][:].rearrange("p m (hb hi wb wi) -> p (m hb) wb hi wi", hb=3, hi=2, wb=3, wi=2),
                 axis=AX.XY, op=ALU.add,
             )
-            nc.vector.tensor_reduce(out=pooled[:, m, 0:1], in_=pooled[:, m, 1:10], axis=AX.X, op=ALU.add)
-            nc.vector.tensor_mul(out=pooled[:, m, 0:46], in0=pooled[:, m, 0:46], in1=level_factor[:])
+            nc.vector.tensor_reduce(out=sums1[:], in_=sums3[:], axis=AX.X, op=ALU.add)
+            nc.vector.tensor_scalar_mul(out=pooleds[b][:, :, 10:46], in0=sums6[b][:], scalar1=9.0 / 16.0)
+            nc.vector.tensor_scalar_mul(out=pooleds[b][:, :, 1:10], in0=sums3[:], scalar1=9.0 / 64.0)
+            nc.vector.tensor_scalar_mul(out=pooleds[b][:, :, 0:1], in0=sums1[:], scalar1=9.0 / 576.0)
+
+        turneds = {}
 
         def turn_value(b):
             turned = psum.tile([P, WIDE], F32, name="bank")
-            for m in range(KEY):
+            for half in range(2):
                 nc.tensor.transpose(
-                    out=turned[:, P * m : P * (m + 1)], in_=pooleds[b][:, m, :], identity=ident[:]
+                    out=turned[:, P * half : P * (half + 1)], in_=pooleds[b][:, 1 + half, :], identity=ident[:]
                 )
             turneds[b] = turned
 
@@ -251,40 +255,37 @@ def tile_afnb_pa_k_kernel(
             value_sb = epi.tile([P, 2 * P], F32, name="value_sb")
             nc.scalar.copy(out=value_sb[:], in_=turneds[b][:, 0 : 2 * P])
             store_queue.dma_start(out=out_0[b], in_=value_sb[0:LOCS, :])
-            store_queue.dma_start(out=out_1[b], in_=pooleds[b][:, KEY, 0:LOCS])
+            store_queue.dma_start(out=out_1[b], in_=pooleds[b][:, 0, 0:LOCS])
+
+        def last_pools(b):
+            pool_blocks(b, 2)
+            pool_coarse(b)
 
         def epilogue_pieces(b):
-            return (
-                [lambda: leave_psum(b)]
-                + [lambda m=m: pool(b, m) for m in range(M_TILES)]
-                + [lambda: turn_value(b), lambda: store(b)]
-            )
+            return [
+                lambda: leave_psum(b),
+                lambda: pool_blocks(b, 0),
+                lambda: pool_blocks(b, 1),
+                lambda: last_pools(b),
+                lambda: turn_value(b),
+                lambda: store(b),
+            ]
 
-        pieces = [turn_vectors, start_key_scale, finish_key_scale]
-        for step in range(UNITS + PE_LAG + 2):
-            if step == PE_LAG:
-                load_scale_rows(wv_plane, wv_scales)
-                load_scale_rows(wk_plane, wk_scales)
-            first_group = step - PE_LAG
-            if 0 <= first_group < GROUPS and first_group % W_CHUNK == 0:
-                load_weight_words(first_group)
+        pieces = []
+        for step in range(UNITS + 1):
+            if step == GROUPS // 2:
+                pieces = [turn_vectors, start_key_scale, finish_key_scale]
             if step + X_AHEAD < UNITS:
-                load_x(step + X_AHEAD)
+                ask(step + X_AHEAD)
             if step < UNITS:
                 regroup(step)
-            if 1 <= step <= UNITS:
+            if step >= 1:
                 quantise(step - 1)
-            narrow_unit = step - PE_LAG - 2
-            wide_unit = step - PE_LAG - 1
-            if 0 <= narrow_unit:
-                multiply(narrow_unit, WIDE, NARROW, "narrow")
-                if narrow_unit % GROUPS == GROUPS - 1:
-                    pieces = epilogue_pieces(narrow_unit // GROUPS)
             if pieces:
                 pieces.pop(0)()
-            if 0 <= wide_unit < UNITS:
-                if wide_unit % GROUPS == 0:
-                    open_banks()
-                multiply(wide_unit, 0, WIDE, "wide")
+            if step >= 1:
+                multiply(step - 1)
+                if step % GROUPS == 0:
+                    pieces = epilogue_pieces(step // GROUPS - 1)
         for piece in pieces:
             piece()

@@ -25,6 +25,7 @@ WIDE = 512
 NARROW = 128
 NARROW_FROM = PIX - NARROW
 TILES = ("key", "value_low", "value_high")
+PASS_ORDER = ("value_low", "value_high", "key")
 LOCS = 110
 EPS = 1e-5
 NINTH = 1.0 / 9.0
@@ -119,15 +120,25 @@ def tile_afnb_pa_k_kernel(
         std = keep.tile([P, 1], F32)
         key_scale = keep.tile([P, 1], F32)
         key_bias = keep.tile([P, 1], F32)
+        bv_rows = keep.tile([P, 2 * P], F32)
         vec_turned = psum.tile([P, WIDE], F32, name="bank")
 
         def turn_vectors():
             vec_rows_f32 = keep.tile([P, P], F32)
             nc.vector.tensor_copy(out=vec_rows_f32[:], in_=vec_rows[:])
             nc.tensor.transpose(out=vec_turned[:, 0:P], in_=vec_rows_f32[:], identity=ident[:])
+            for half in range(2):
+                nc.tensor.matmul(
+                    out=vec_turned[:, P * (1 + half) : P * (2 + half)],
+                    lhsT=ident[:, 5 + half : 6 + half].to_broadcast([P, P]),
+                    rhs=vec_rows_f32[:],
+                    start=True,
+                    stop=True,
+                )
 
         def start_key_scale():
             nc.vector.tensor_copy(out=cols[:], in_=vec_turned[:, 0:8])
+            nc.vector.tensor_copy(out=bv_rows[:], in_=vec_turned[:, P : 3 * P])
             nc.vector.tensor_scalar_mul(out=cols_ninth[:], in0=cols[:], scalar1=NINTH)
             nc.vector.tensor_scalar_add(out=std[:], in0=cols[:, 4:5], scalar1=EPS)
             nc.scalar.sqrt(out=std[:], in_=std[:])
@@ -176,7 +187,7 @@ def tile_afnb_pa_k_kernel(
 
         def multiply(u):
             b, g = divmod(u, GROUPS)
-            for name in TILES:
+            for name in PASS_ORDER:
                 words, plane = weights(name, g)
                 for window, first, width in (("wide", 0, WIDE), ("narrow", NARROW_FROM, NARROW)):
                     if g == 0:
@@ -194,38 +205,36 @@ def tile_afnb_pa_k_kernel(
         fulls = {}
 
         def leave_psum(b):
-            full = epi.tile([P, len(TILES), PIX], F32, name="full")
-            for m, name in enumerate(TILES):
-                for dst, src in (
-                    (full[:, m, 0:WIDE], sums[b, name, "wide"][:, 0:WIDE]),
-                    (full[:, m, WIDE:PIX], sums[b, name, "narrow"][:, WIDE - NARROW_FROM : NARROW]),
-                ):
-                    if name == "key":
-                        nc.scalar.activation(
-                            out=dst, in_=src, func=ACT.Relu, bias=key_bias[:, 0:1], scale=key_scale[:, 0:1]
-                        )
-                    else:
-                        nc.scalar.activation(
-                            out=dst, in_=src, func=ACT.Identity, bias=cols_ninth[:, 4 + m : 5 + m], scale=NINTH
-                        )
+            full = epi.tile([P, PIX], F32, name="full")
+            for dst, src in (
+                (full[:, 0:WIDE], sums[b, "key", "wide"][:, 0:WIDE]),
+                (full[:, WIDE:PIX], sums[b, "key", "narrow"][:, WIDE - NARROW_FROM : NARROW]),
+            ):
+                nc.scalar.activation(
+                    out=dst, in_=src, func=ACT.Relu, bias=key_bias[:, 0:1], scale=key_scale[:, 0:1]
+                )
             fulls[b] = full
 
         sums6 = {}
 
         def pool_blocks(b, m):
-            if m == 0:
+            if b not in sums6:
                 sums6[b] = epi.tile([P, len(TILES), 36], F32, name="sums6")
-            image = fulls[b][:, m, :]
-            nc.vector.tensor_reduce(
-                out=pooleds[b][:, m, 46:110].rearrange("p (hb wb) -> p hb wb", hb=8),
-                in_=image.rearrange("p (hb hi wb wi) -> p hb wb hi wi", hb=8, hi=3, wb=8, wi=3),
-                axis=AX.XY, op=ALU.add,
-            )
-            nc.vector.tensor_reduce(
-                out=sums6[b][:, m, :].rearrange("p (hb wb) -> p hb wb", hb=6),
-                in_=image.rearrange("p (hb hi wb wi) -> p hb wb hi wi", hb=6, hi=4, wb=6, wi=4),
-                axis=AX.XY, op=ALU.add,
-            )
+            for side, out in ((3, pooleds[b][:, m, 46:110]), (4, sums6[b][:, m, :])):
+                across = SIDE // side
+                if m == 0:
+                    parts = ((fulls[b][:, :], 0, across),)
+                else:
+                    parts = (
+                        (sums[b, TILES[m], "wide"][:, 0 : (across - 1) * side * SIDE], 0, across - 1),
+                        (sums[b, TILES[m], "narrow"][:, NARROW - side * SIDE : NARROW], across - 1, 1),
+                    )
+                for in_, first, rows in parts:
+                    nc.vector.tensor_reduce(
+                        out=out[:, first * across : (first + rows) * across].rearrange("p (hb wb) -> p hb wb", hb=rows),
+                        in_=in_.rearrange("p (hb hi wb wi) -> p hb wb hi wi", hb=rows, hi=side, wb=across, wi=side),
+                        axis=AX.XY, op=ALU.add,
+                    )
 
         def pool_coarse(b):
             sums3 = epi.tile([P, len(TILES), 9], F32, name="sums3")
@@ -235,8 +244,8 @@ def tile_afnb_pa_k_kernel(
                 in_=sums6[b][:].rearrange("p m (hb hi wb wi) -> p (m hb) wb hi wi", hb=3, hi=2, wb=3, wi=2),
                 axis=AX.XY, op=ALU.add,
             )
-            nc.vector.tensor_reduce(out=sums1[:], in_=sums3[:], axis=AX.X, op=ALU.add)
-            nc.vector.tensor_scalar_mul(out=pooleds[b][:, :, 10:46], in0=sums6[b][:], scalar1=9.0 / 16.0)
+            nc.scalar.mul(out=pooleds[b][:, :, 10:46], in_=sums6[b][:], mul=9.0 / 16.0)
+            nc.vector.tensor_reduce(out=sums1[:], in_=sums6[b][:], axis=AX.X, op=ALU.add)
             nc.vector.tensor_scalar_mul(out=pooleds[b][:, :, 1:10], in0=sums3[:], scalar1=9.0 / 64.0)
             nc.vector.tensor_scalar_mul(out=pooleds[b][:, :, 0:1], in0=sums1[:], scalar1=9.0 / 576.0)
 
@@ -252,20 +261,26 @@ def tile_afnb_pa_k_kernel(
 
         def store(b):
             store_queue = nc.sync if b == BATCH - 1 else nc.gpsimd
-            value_sb = epi.tile([P, 2 * P], F32, name="value_sb")
-            nc.scalar.copy(out=value_sb[:], in_=turneds[b][:, 0 : 2 * P])
-            store_queue.dma_start(out=out_0[b], in_=value_sb[0:LOCS, :])
             store_queue.dma_start(out=out_1[b], in_=pooleds[b][:, 0, 0:LOCS])
+            value_sb = epi.tile([P, 2 * P], F32, name="value_sb")
+            nc.vector.scalar_tensor_tensor(
+                out=value_sb[:], in0=turneds[b][:, 0 : 2 * P], scalar=NINTH, in1=bv_rows[:],
+                op0=ALU.mult, op1=ALU.add,
+            )
+            store_queue.dma_start(out=out_0[b], in_=value_sb[0:LOCS, :])
+
+        def first_pools(b):
+            leave_psum(b)
+            pool_blocks(b, 1)
+            pool_blocks(b, 2)
 
         def last_pools(b):
-            pool_blocks(b, 2)
+            pool_blocks(b, 0)
             pool_coarse(b)
 
         def epilogue_pieces(b):
             return [
-                lambda: leave_psum(b),
-                lambda: pool_blocks(b, 0),
-                lambda: pool_blocks(b, 1),
+                lambda: first_pools(b),
                 lambda: last_pools(b),
                 lambda: turn_value(b),
                 lambda: store(b),

@@ -220,7 +220,7 @@ def tile_afnb_pa_k_kernel(
         def pool_blocks(b, m):
             if b not in sums6:
                 sums6[b] = epi.tile([P, len(TILES), 36], F32, name="sums6")
-            for side, out in ((3, pooleds[b][:, m, 46:110]), (4, sums6[b][:, m, :])):
+            for side, out in ((4, sums6[b][:, m, :]), (3, pooleds[b][:, m, 46:110])):
                 across = SIDE // side
                 if m == 0:
                     parts = ((fulls[b][:, :], 0, across),)
@@ -260,7 +260,7 @@ def tile_afnb_pa_k_kernel(
             turneds[b] = turned
 
         def store(b):
-            store_queue = nc.sync if b == BATCH - 1 else nc.gpsimd
+            store_queue = nc.sync
             store_queue.dma_start(out=out_1[b], in_=pooleds[b][:, 0, 0:LOCS])
             value_sb = epi.tile([P, 2 * P], F32, name="value_sb")
             nc.vector.scalar_tensor_tensor(

@@ -216,38 +216,47 @@ def tile_afnb_pa_k_kernel(
             fulls[b] = full
 
         sums6 = {}
+        sums3 = {}
+        sums1 = {}
 
-        def pool_blocks(b, m):
-            if b not in sums6:
-                sums6[b] = epi.tile([P, len(TILES), 36], F32, name="sums6")
-            for side, out in ((4, sums6[b][:, m, :]), (3, pooleds[b][:, m, 46:110])):
-                across = SIDE // side
-                if m == 0:
-                    parts = ((fulls[b][:, :], 0, across),)
-                else:
-                    parts = (
-                        (sums[b, TILES[m], "wide"][:, 0 : (across - 1) * side * SIDE], 0, across - 1),
-                        (sums[b, TILES[m], "narrow"][:, NARROW - side * SIDE : NARROW], across - 1, 1),
-                    )
-                for in_, first, rows in parts:
-                    nc.vector.tensor_reduce(
-                        out=out[:, first * across : (first + rows) * across].rearrange("p (hb wb) -> p hb wb", hb=rows),
-                        in_=in_.rearrange("p (hb hi wb wi) -> p hb wb hi wi", hb=rows, hi=side, wb=across, wi=side),
-                        axis=AX.XY, op=ALU.add,
-                    )
-
-        def pool_coarse(b):
-            sums3 = epi.tile([P, len(TILES), 9], F32, name="sums3")
-            sums1 = epi.tile([P, len(TILES), 1], F32, name="sums1")
+        def reduce_blocks(b, m, side, part):
+            across = SIDE // side
+            out = pooleds[b][:, m, 46:110] if side == 3 else sums6[b][:, m, :]
+            if part == "all":
+                in_, first, rows = fulls[b][:, :], 0, across
+            elif part == "wide":
+                in_, first, rows = sums[b, TILES[m], "wide"][:, 0 : (across - 1) * side * SIDE], 0, across - 1
+            else:
+                in_, first, rows = sums[b, TILES[m], "narrow"][:, NARROW - side * SIDE : NARROW], across - 1, 1
             nc.vector.tensor_reduce(
-                out=sums3[:].rearrange("p m (hb wb) -> p (m hb) wb", hb=3),
+                out=out[:, first * across : (first + rows) * across].rearrange("p (hb wb) -> p hb wb", hb=rows),
+                in_=in_.rearrange("p (hb hi wb wi) -> p hb wb hi wi", hb=rows, hi=side, wb=across, wi=side),
+                axis=AX.XY, op=ALU.add,
+            )
+
+        def pool(b):
+            sums6[b] = epi.tile([P, len(TILES), 36], F32, name="sums6")
+            sums3[b] = epi.tile([P, len(TILES), 9], F32, name="sums3")
+            sums1[b] = epi.tile([P, len(TILES), 1], F32, name="sums1")
+            leave_psum(b)
+            reduce_blocks(b, 1, 4, "wide")
+            reduce_blocks(b, 1, 4, "narrow")
+            reduce_blocks(b, 2, 4, "wide")
+            reduce_blocks(b, 2, 4, "narrow")
+            reduce_blocks(b, 1, 3, "wide")
+            reduce_blocks(b, 0, 4, "all")
+            reduce_blocks(b, 2, 3, "wide")
+            nc.vector.tensor_reduce(
+                out=sums3[b][:].rearrange("p m (hb wb) -> p (m hb) wb", hb=3),
                 in_=sums6[b][:].rearrange("p m (hb hi wb wi) -> p (m hb) wb hi wi", hb=3, hi=2, wb=3, wi=2),
                 axis=AX.XY, op=ALU.add,
             )
             nc.scalar.mul(out=pooleds[b][:, :, 10:46], in_=sums6[b][:], mul=9.0 / 16.0)
-            nc.vector.tensor_reduce(out=sums1[:], in_=sums6[b][:], axis=AX.X, op=ALU.add)
-            nc.vector.tensor_scalar_mul(out=pooleds[b][:, :, 1:10], in0=sums3[:], scalar1=9.0 / 64.0)
-            nc.vector.tensor_scalar_mul(out=pooleds[b][:, :, 0:1], in0=sums1[:], scalar1=9.0 / 576.0)
+            reduce_blocks(b, 1, 3, "narrow")
+            nc.vector.tensor_reduce(out=sums1[b][:], in_=sums6[b][:], axis=AX.X, op=ALU.add)
+            reduce_blocks(b, 2, 3, "narrow")
+            nc.vector.tensor_scalar_mul(out=pooleds[b][:, :, 1:10], in0=sums3[b][:], scalar1=9.0 / 64.0)
+            nc.vector.tensor_scalar_mul(out=pooleds[b][:, :, 0:1], in0=sums1[b][:], scalar1=9.0 / 576.0)
 
         turneds = {}
 
@@ -269,20 +278,14 @@ def tile_afnb_pa_k_kernel(
             )
             store_queue.dma_start(out=out_0[b], in_=value_sb[0:LOCS, :])
 
-        def first_pools(b):
-            leave_psum(b)
-            pool_blocks(b, 1)
-            pool_blocks(b, 2)
-
-        def last_pools(b):
-            pool_blocks(b, 0)
-            pool_coarse(b)
+        def turn_and_finish_key(b):
+            turn_value(b)
+            reduce_blocks(b, 0, 3, "all")
 
         def epilogue_pieces(b):
             return [
-                lambda: first_pools(b),
-                lambda: last_pools(b),
-                lambda: turn_value(b),
+                lambda: pool(b),
+                lambda: turn_and_finish_key(b),
                 lambda: store(b),
             ]
 

@@ -31,7 +31,7 @@ EPS = 1e-5
 NINTH = 1.0 / 9.0
 
 RUN = 4
-VECTOR_PIX = 256
+VECTOR_PIX = (288, 256)
 RAW_BUFS = 6
 X_AHEAD = RAW_BUFS - 1
 GROUPED_BUFS = 4
@@ -88,8 +88,10 @@ def tile_afnb_pa_k_kernel(
                 load_scale_rows(wv_plane, wv_scales)
             if u == 1:
                 load_scale_rows(wk_plane, wk_scales)
-            if u < GROUPS and u % W_CHUNK == 0:
-                load_weight_words(u)
+            if u == 0:
+                load_weight_words(0)
+            elif u <= GROUPS and u % W_CHUNK == 1 and u > 1:
+                load_weight_words(u - 1)
 
         vec_rows = keep.tile([P, P], BF16)
         nc.gpsimd.memset(vec_rows[:], 0.0)
@@ -160,7 +162,7 @@ def tile_afnb_pa_k_kernel(
             grouped = grouped_pool.tile([P, PIX, PACK], BF16, name="grouped", align_bytes=64)
             src = raws[u][:].rearrange("p j (c i) -> p c j i", i=RUN)
             dst = grouped[:].rearrange("p (c i) j -> p c j i", i=RUN)
-            cut = VECTOR_PIX // RUN
+            cut = VECTOR_PIX[u // GROUPS] // RUN
             nc.vector.tensor_copy(out=dst[:, :cut], in_=src[:, :cut])
             nc.scalar.copy(out=dst[:, cut:], in_=src[:, cut:])
             groupeds[u] = grouped
@@ -270,7 +272,6 @@ def tile_afnb_pa_k_kernel(
 
         def store(b):
             store_queue = nc.sync
-            store_queue.dma_start(out=out_1[b], in_=pooleds[b][:, 0, 0:LOCS])
             value_sb = epi.tile([P, 2 * P], F32, name="value_sb")
             nc.vector.scalar_tensor_tensor(
                 out=value_sb[:], in0=turneds[b][:, 0 : 2 * P], scalar=NINTH, in1=bv_rows[:],
@@ -278,9 +279,14 @@ def tile_afnb_pa_k_kernel(
             )
             store_queue.dma_start(out=out_0[b], in_=value_sb[0:LOCS, :])
 
+        def finish_key(b):
+            reduce_blocks(b, 0, 3, "all")
+            nc.sync.dma_start(out=out_1[b], in_=pooleds[b][:, 0, 0:LOCS])
+
         def turn_and_finish_key(b):
             turn_value(b)
-            reduce_blocks(b, 0, 3, "all")
+            if b == BATCH - 1:
+                finish_key(b)
 
         def epilogue_pieces(b):
             return [
@@ -299,6 +305,8 @@ def tile_afnb_pa_k_kernel(
                 regroup(step)
             if step >= 1:
                 quantise(step - 1)
+            if step == UNITS:
+                finish_key(0)
             if pieces:
                 pieces.pop(0)()
             if step >= 1:

from contextlib import ExitStack

import concourse.mybir as mybir
from concourse.masks import make_identity

F32 = mybir.dt.float32
BF16 = mybir.dt.bfloat16
I32 = mybir.dt.int32
U32 = mybir.dt.uint32
U8 = mybir.dt.uint8
FP8X4 = mybir.dt.float8_e4m3fn_x4
FP4X4 = mybir.dt.float4_e2m1fn_x4
ACT = mybir.ActivationFunctionType
ALU = mybir.AluOpType
AX = mybir.AxisListType

P = 128
PACK = 4
BATCH = 2
GROUPS = 16
UNITS = BATCH * GROUPS
SIDE = 24
PIX = SIDE * SIDE
WIDE = 512
NARROW = 128
NARROW_FROM = PIX - NARROW
TILES = ("key", "value_low", "value_high")
PASS_ORDER = ("value_low", "value_high", "key")
LOCS = 110
EPS = 1e-5
NINTH = 1.0 / 9.0

RUN = 4
VECTOR_PIX = (288, 256)
RAW_BUFS = 6
X_AHEAD = RAW_BUFS - 1
GROUPED_BUFS = 4
W_CHUNK = 2
BANKS = 8

FLOPS = 2 * BATCH * PIX * 8192 * (256 + 128)


def tile_afnb_pa_k_kernel(
    tc, low_feats, wk_words, wk_scales, bk, gk, bek, mk, vk, wv_words, wv_scales, bv, out_0, out_1
):
    nc = tc.nc
    x_units = low_feats.rearrange("b (g p j) h w -> (b g) p (j h w)", p=P, j=PACK)

    with ExitStack() as ctx:
        keep = ctx.enter_context(tc.tile_pool(name="keep", bufs=1))
        raw_pool = ctx.enter_context(tc.tile_pool(name="raw", bufs=RAW_BUFS))
        grouped_pool = ctx.enter_context(tc.tile_pool(name="grouped", bufs=GROUPED_BUFS))
        epi = ctx.enter_context(tc.tile_pool(name="epi", bufs=2))
        psum = ctx.enter_context(tc.psum_pool(name="psum", bufs=BANKS))
        ctx.enter_context(tc.manual_schedule())

        x_codes = keep.tile([P, UNITS, PIX], U32, align_bytes=64)
        x_scales = keep.tile([P, UNITS, PIX], U8, align_bytes=64)
        wv_sb = keep.tile([P, GROUPS, 2 * 256], U8, align_bytes=64)
        wk_sb = keep.tile([P, GROUPS, 2 * 128], U8, align_bytes=64)
        wv_plane = keep.tile([P, GROUPS, 256], U8, align_bytes=64)
        wk_plane = keep.tile([P, GROUPS, 128], U8, align_bytes=64)

        def load_scale_rows(plane, scales):
            rows = scales.rearrange("g (q r) n -> r q g n", r=4)
            for r in range(4):
                nc.sync.dma_start(out=plane[r:P:32, :, :].bitcast(I32), in_=rows[r].bitcast(I32))

        def load_weight_words(g0):
            gs = slice(g0, g0 + W_CHUNK)
            nc.sync.dma_start(
                out=wv_sb[:, gs, :].bitcast(I32),
                in_=wv_words[gs].rearrange("g p n -> p g n").bitcast(I32),
            )
            nc.sync.dma_start(
                out=wk_sb[:, gs, :].bitcast(I32),
                in_=wk_words[gs].rearrange("g p n -> p g n").bitcast(I32),
            )

        raws = {}

        def ask(u):
            raw = raw_pool.tile([P, PACK, PIX], BF16, name="raw")
            nc.sync.dma_start(out=raw[:].rearrange("p j w -> p (j w)"), in_=x_units[u])
            raws[u] = raw
            if u == 0:
                load_scale_rows(wv_plane, wv_scales)
            if u == 1:
                load_scale_rows(wk_plane, wk_scales)
            if u == 0:
                load_weight_words(0)
            elif u <= GROUPS and u % W_CHUNK == 1 and u > 1:
                load_weight_words(u - 1)

        vec_rows = keep.tile([P, P], BF16)
        nc.gpsimd.memset(vec_rows[:], 0.0)
        for row, vec in enumerate((bk, gk, bek, mk, vk)):
            nc.gpsimd.dma_start(out=vec_rows[row : row + 1, :], in_=vec.rearrange("(o c) -> o c", o=1))
        nc.gpsimd.dma_start(out=vec_rows[5:7, :], in_=bv.rearrange("(o c) -> o c", o=2))

        nc.vector.memset(wv_plane[:].rearrange("p g n -> p (g n)").bitcast(I32), 0)
        nc.vector.memset(wk_plane[:].rearrange("p g n -> p (g n)").bitcast(I32), 0)
        for u in range(X_AHEAD):
            ask(u)

        one = keep.tile([P, 1], F32)
        nc.vector.memset(one[:], 1.0)
        nc.scalar.sqrt(out=one[:], in_=one[:])

        ident = keep.tile([P, P], F32)
        make_identity(nc, ident[:])

        pooleds = []
        for b in range(BATCH):
            pooled = keep.tile([P, len(TILES), P], F32, name="pooled%d" % b)
            nc.gpsimd.memset(pooled[:], 0.0)
            pooleds.append(pooled)

        cols = keep.tile([P, 8], F32)
        cols_ninth = keep.tile([P, 8], F32)
        std = keep.tile([P, 1], F32)
        key_scale = keep.tile([P, 1], F32)
        key_bias = keep.tile([P, 1], F32)
        bv_rows = keep.tile([P, 2 * P], F32)
        vec_turned = psum.tile([P, WIDE], F32, name="bank")

        def turn_vectors():
            vec_rows_f32 = keep.tile([P, P], F32)
            nc.vector.tensor_copy(out=vec_rows_f32[:], in_=vec_rows[:])
            nc.tensor.transpose(out=vec_turned[:, 0:P], in_=vec_rows_f32[:], identity=ident[:])
            for half in range(2):
                nc.tensor.matmul(
                    out=vec_turned[:, P * (1 + half) : P * (2 + half)],
                    lhsT=ident[:, 5 + half : 6 + half].to_broadcast([P, P]),
                    rhs=vec_rows_f32[:],
                    start=True,
                    stop=True,
                )

        def start_key_scale():
            nc.vector.tensor_copy(out=cols[:], in_=vec_turned[:, 0:8])
            nc.vector.tensor_copy(out=bv_rows[:], in_=vec_turned[:, P : 3 * P])
            nc.vector.tensor_scalar_mul(out=cols_ninth[:], in0=cols[:], scalar1=NINTH)
            nc.vector.tensor_scalar_add(out=std[:], in0=cols[:, 4:5], scalar1=EPS)
            nc.scalar.sqrt(out=std[:], in_=std[:])

        def finish_key_scale():
            inv_std = keep.tile([P, 1], F32)
            nc.vector.reciprocal(out=inv_std[:], in_=std[:])
            nc.vector.tensor_mul(out=key_scale[:], in0=cols_ninth[:, 1:2], in1=inv_std[:])
            bk_less_mk = keep.tile([P, 1], F32)
            nc.vector.tensor_sub(out=bk_less_mk[:], in0=cols[:, 0:1], in1=cols[:, 3:4])
            nc.vector.scalar_tensor_tensor(
                out=key_bias[:], in0=bk_less_mk[:], scalar=key_scale[:, 0:1], in1=cols_ninth[:, 2:3],
                op0=ALU.mult, op1=ALU.add,
            )

        groupeds = {}

        def regroup(u):
            grouped = grouped_pool.tile([P, PIX, PACK], BF16, name="grouped", align_bytes=64)
            src = raws[u][:].rearrange("p j (c i) -> p c j i", i=RUN)
            dst = grouped[:].rearrange("p (c i) j -> p c j i", i=RUN)
            cut = VECTOR_PIX[u // GROUPS] // RUN
            nc.vector.tensor_copy(out=dst[:, :cut], in_=src[:, :cut])
            nc.scalar.copy(out=dst[:, cut:], in_=src[:, cut:])
            groupeds[u] = grouped

        def quantise(u):
            flat = groupeds[u][:].rearrange("p w j -> p (w j)")
            for lo, hi in ((0, WIDE), (WIDE, PIX)):
                nc.vector.quantize_mx(
                    out=x_codes[:, u, lo:hi].bitcast(FP8X4),
                    scales=x_scales[:, u, lo:hi],
                    in_=flat[:, PACK * lo : PACK * hi],
                )

        def weights(name, g):
            if name == "key":
                return wk_sb[:, g, :].bitcast(FP4X4), wk_plane[:, g, :]
            half = TILES.index(name) - 1
            return (
                wv_sb[:, g, 2 * P * half : 2 * P * (half + 1)].bitcast(FP4X4),
                wv_plane[:, g, P * half : P * (half + 1)],
            )

        sums = {}

        def multiply(u):
            b, g = divmod(u, GROUPS)
            for name in PASS_ORDER:
                words, plane = weights(name, g)
                for window, first, width in (("wide", 0, WIDE), ("narrow", NARROW_FROM, NARROW)):
                    if g == 0:
                        sums[b, name, window] = psum.tile([P, WIDE], F32, name="bank")
                    nc.tensor.matmul_mx(
                        out=sums[b, name, window][:, 0:width],
                        lhsT=words,
                        lhsT_scale=plane,
                        rhs=x_codes[:, u, first : first + width].bitcast(FP8X4),
                        rhs_scale=x_scales[:, u, first : first + width],
                        start=(g == 0),
                        stop=(g == GROUPS - 1),
                    )

        fulls = {}

        def leave_psum(b):
            full = epi.tile([P, PIX], F32, name="full")
            for dst, src in (
                (full[:, 0:WIDE], sums[b, "key", "wide"][:, 0:WIDE]),
                (full[:, WIDE:PIX], sums[b, "key", "narrow"][:, WIDE - NARROW_FROM : NARROW]),
            ):
                nc.scalar.activation(
                    out=dst, in_=src, func=ACT.Relu, bias=key_bias[:, 0:1], scale=key_scale[:, 0:1]
                )
            fulls[b] = full

        sums6 = {}
        sums3 = {}
        sums1 = {}

        def reduce_blocks(b, m, side, part):
            across = SIDE // side
            out = pooleds[b][:, m, 46:110] if side == 3 else sums6[b][:, m, :]
            if part == "all":
                in_, first, rows = fulls[b][:, :], 0, across
            elif part == "wide":
                in_, first, rows = sums[b, TILES[m], "wide"][:, 0 : (across - 1) * side * SIDE], 0, across - 1
            else:
                in_, first, rows = sums[b, TILES[m], "narrow"][:, NARROW - side * SIDE : NARROW], across - 1, 1
            nc.vector.tensor_reduce(
                out=out[:, first * across : (first + rows) * across].rearrange("p (hb wb) -> p hb wb", hb=rows),
                in_=in_.rearrange("p (hb hi wb wi) -> p hb wb hi wi", hb=rows, hi=side, wb=across, wi=side),
                axis=AX.XY, op=ALU.add,
            )

        def pool(b):
            sums6[b] = epi.tile([P, len(TILES), 36], F32, name="sums6")
            sums3[b] = epi.tile([P, len(TILES), 9], F32, name="sums3")
            sums1[b] = epi.tile([P, len(TILES), 1], F32, name="sums1")
            leave_psum(b)
            reduce_blocks(b, 1, 4, "wide")
            reduce_blocks(b, 1, 4, "narrow")
            reduce_blocks(b, 2, 4, "wide")
            reduce_blocks(b, 2, 4, "narrow")
            reduce_blocks(b, 1, 3, "wide")
            reduce_blocks(b, 0, 4, "all")
            reduce_blocks(b, 2, 3, "wide")
            nc.vector.tensor_reduce(
                out=sums3[b][:].rearrange("p m (hb wb) -> p (m hb) wb", hb=3),
                in_=sums6[b][:].rearrange("p m (hb hi wb wi) -> p (m hb) wb hi wi", hb=3, hi=2, wb=3, wi=2),
                axis=AX.XY, op=ALU.add,
            )
            nc.scalar.mul(out=pooleds[b][:, :, 10:46], in_=sums6[b][:], mul=9.0 / 16.0)
            reduce_blocks(b, 1, 3, "narrow")
            nc.vector.tensor_reduce(out=sums1[b][:], in_=sums6[b][:], axis=AX.X, op=ALU.add)
            reduce_blocks(b, 2, 3, "narrow")
            nc.vector.tensor_scalar_mul(out=pooleds[b][:, :, 1:10], in0=sums3[b][:], scalar1=9.0 / 64.0)
            nc.vector.tensor_scalar_mul(out=pooleds[b][:, :, 0:1], in0=sums1[b][:], scalar1=9.0 / 576.0)

        turneds = {}

        def turn_value(b):
            turned = psum.tile([P, WIDE], F32, name="bank")
            for half in range(2):
                nc.tensor.transpose(
                    out=turned[:, P * half : P * (half + 1)], in_=pooleds[b][:, 1 + half, :], identity=ident[:]
                )
            turneds[b] = turned

        def store(b):
            store_queue = nc.sync
            value_sb = epi.tile([P, 2 * P], F32, name="value_sb")
            nc.vector.scalar_tensor_tensor(
                out=value_sb[:], in0=turneds[b][:, 0 : 2 * P], scalar=NINTH, in1=bv_rows[:],
                op0=ALU.mult, op1=ALU.add,
            )
            store_queue.dma_start(out=out_0[b], in_=value_sb[0:LOCS, :])

        def finish_key(b):
            reduce_blocks(b, 0, 3, "all")
            nc.sync.dma_start(out=out_1[b], in_=pooleds[b][:, 0, 0:LOCS])

        def turn_and_finish_key(b):
            turn_value(b)
            if b == BATCH - 1:
                finish_key(b)

        def epilogue_pieces(b):
            return [
                lambda: pool(b),
                lambda: turn_and_finish_key(b),
                lambda: store(b),
            ]

        pieces = []
        for step in range(UNITS + 1):
            if step == GROUPS // 2:
                pieces = [turn_vectors, start_key_scale, finish_key_scale]
            if step + X_AHEAD < UNITS:
                ask(step + X_AHEAD)
            if step < UNITS:
                regroup(step)
            if step >= 1:
                quantise(step - 1)
            if step == UNITS:
                finish_key(0)
            if pieces:
                pieces.pop(0)()
            if step >= 1:
                multiply(step - 1)
                if step % GROUPS == 0:
                    pieces = epilogue_pieces(step // GROUPS - 1)
        for piece in pieces:
            piece()
